import numpy as np
import ml_dtypes


def mxq(x, axis, fmt="e4m3"):
    dtype, down = {"e4m3": (ml_dtypes.float8_e4m3fn, 7), "e5m2": (ml_dtypes.float8_e5m2, 14)}[fmt]
    v = np.moveaxis(np.asarray(x, np.float32).astype(ml_dtypes.bfloat16).astype(np.float64), axis, -1)
    blocks = v.reshape(v.shape[:-1] + (-1, 32))
    amax = np.abs(blocks).max(-1, keepdims=True)
    byte = np.maximum(np.where(amax > 0, np.frexp(amax)[1] - 1 + 127, 0) - down, 1)
    scale = np.exp2(byte - 127.0)
    codes = (blocks / scale).astype(np.float32).astype(dtype).astype(np.float64)
    return np.moveaxis((codes * scale).reshape(v.shape), -1, axis)


WIDE = False


def mx_kscale(k):
    if not WIDE:
        return np.ones(k)
    levels = np.array([10, -10, 5, -5, 0])
    a = np.random.permutation(np.resize(levels, k // 512 * 4)).reshape(k // 512, 4)
    idx = np.arange(k)
    return np.exp2(a[idx // 512, idx % 128 // 32])


BF16 = ml_dtypes.bfloat16


def bf(x):
    return np.asarray(x, np.float32).astype(BF16)


def f64(x):
    return np.asarray(x).astype(np.float64)


E2M1 = np.array([0.0, 0.5, 1.0, 1.5, 2.0, 3.0, 4.0, 6.0, -0.0, -0.5, -1.0, -1.5, -2.0, -3.0, -4.0, -6.0])


def pack_weight(w, fmt):
    k, n = w.shape
    w = f64(bf(w)).reshape(k // 32, 32, n)
    amax = np.abs(w).max(1)
    if fmt == "e4m3":
        byte = np.frexp(amax)[1] - 1 + 127 - 7
    else:
        mant, ex = np.frexp(amax / 6.0)
        byte = np.where(mant > 0.5, ex, ex - 1) + 127
    byte = np.clip(np.where(amax > 0, byte, 1), 1, 254)
    scaled = (w * np.exp2(127.0 - byte)[:, None, :]).reshape(k, n).astype(np.float32)
    by_word = np.ascontiguousarray(scaled.reshape(k // 512, 128, 4, n).transpose(0, 1, 3, 2))
    if fmt == "e4m3":
        words = by_word.astype(ml_dtypes.float8_e4m3fn).view(np.uint8)
    else:
        c = by_word.astype(ml_dtypes.float4_e2m1fn).view(np.uint8) & 0xF
        words = c[..., 0::2] | (c[..., 1::2] << 4)
    return np.ascontiguousarray(words), np.ascontiguousarray(byte.astype(np.uint8).reshape(k // 512, 16, n))


def unpack_weight(words, scales, fmt):
    g, p, n, _ = words.shape
    if fmt == "e4m3":
        vals = np.ascontiguousarray(words).view(ml_dtypes.float8_e4m3fn).astype(np.float64)
    else:
        nib = np.empty((g, p, n, 4), np.uint8)
        nib[..., 0::2] = words & 0xF
        nib[..., 1::2] = words >> 4
        vals = E2M1[nib]
    vals = vals * np.repeat(np.exp2(scales.astype(np.float64) - 127.0), 8, axis=1)[..., None]
    return vals.transpose(0, 1, 3, 2).reshape(g * 512, n)


B, C, NB, BW, T, EMB = 1, 2, 2, 1024, 128, 3072
F = NB * BW
FEAT = C * BW * 2
EPS = 1e-5


def setup_inputs():
    s = mx_kscale(FEAT)
    amp = np.exp2(np.random.uniform(-9.0, 1.0, (B, 1, 1, T)))
    x_real = bf(amp * (np.random.standard_normal((B, C, F, T)) + 0.6))
    x_imag = bf(amp * (np.random.standard_normal((B, C, F, T)) + 0.2))
    ln_w = bf((1.0 + 0.1 * np.random.standard_normal((NB, FEAT))) * s)
    ln_b = bf(0.1 * np.random.standard_normal((NB, FEAT)) * s)
    fc_w = np.random.standard_normal((NB, FEAT, EMB)) / np.sqrt(FEAT) / s[:, None]
    fc_w_words, fc_w_scales = pack_weight(fc_w.reshape(-1, EMB), "e4m3")
    fc_b = bf(0.3 * np.random.standard_normal((NB, EMB)))
    return {"x_real": x_real,
            "x_imag": x_imag,
            "ln_w": ln_w,
            "ln_b": ln_b,
            "fc_w_words": fc_w_words,
            "fc_w_scales": fc_w_scales,
            "fc_b": fc_b}


def reference(x_real, x_imag, ln_w, ln_b, fc_w_words, fc_w_scales, fc_b):
    x_real, x_imag, ln_w, ln_b, fc_b = f64(x_real), f64(x_imag), f64(ln_w), f64(ln_b), f64(fc_b)
    b, c, f, t = x_real.shape
    nb, feat = ln_w.shape
    bw = f // nb
    xr = np.transpose(x_real, (0, 3, 1, 2)).reshape(b, t, c, nb, bw)
    xi = np.transpose(x_imag, (0, 3, 1, 2)).reshape(b, t, c, nb, bw)
    xb = np.stack([xr, xi], axis=-1)
    xb = np.transpose(xb, (0, 3, 1, 2, 4, 5))
    xb = xb.reshape(b, nb, t, feat)
    mean = np.mean(xb, axis=-1, keepdims=True)
    var = np.mean(np.square(xb - mean), axis=-1, keepdims=True)
    xn = (xb - mean) * (1.0 / np.sqrt(var + EPS))
    xn = xn * ln_w[None, :, None, :] + ln_b[None, :, None, :]
    z = (mxq(xn, 3, "e4m3") @ unpack_weight(fc_w_words, fc_w_scales, "e4m3").reshape(NB, FEAT, EMB)[None]) + fc_b[None, :, None, :]
    return z

@@ -1,0 +1,266 @@
+from contextlib import ExitStack
+
+import concourse.mybir as mybir
+from concourse.masks import make_identity
+
+F32 = mybir.dt.float32
+BF16 = mybir.dt.bfloat16
+I32 = mybir.dt.int32
+U32 = mybir.dt.uint32
+U8 = mybir.dt.uint8
+FP8X4 = mybir.dt.float8_e4m3fn_x4
+ALU = mybir.AluOpType
+ACT = mybir.ActivationFunctionType
+
+P = 128
+PACK = 4
+K_PASS = P * PACK
+BANDS = 2
+CHANNELS = 2
+PARTS = 2
+BINS = 1024
+FRAMES = 128
+FEAT = CHANNELS * BINS * PARTS
+EMB = 3072
+EPS = 1e-5
+GROUPS = FEAT // K_PASS
+GROUPS_C = GROUPS // CHANNELS
+SLICES_C = 2 * GROUPS_C
+N_TILE = 512
+N_TILES = EMB // N_TILE
+PLANES = 4
+QUADRANTS = 4
+W_BUFS = 10
+STORE_TILES = 2
+
+GAIN_ROW = 0
+SHIFT_ROW = BANDS * GROUPS
+FC_B_ROW = 2 * BANDS * GROUPS
+
+FLOPS = 2 * BANDS * FRAMES * FEAT * EMB
+
+
+def spread_over_partitions(nc, row, column, ident):
+    nc.tensor.matmul(out=row, lhsT=column.to_broadcast([P, P]), rhs=ident, start=True, stop=True)
+
+
+def load_band(nc, pool, x_real, x_imag, band):
+    raw = pool.tile([P, PARTS, CHANNELS, SLICES_C, FRAMES], BF16, tag="raw", name="raw%d" % band)
+    for r, x_part in enumerate((x_real, x_imag)):
+        for c in range(CHANNELS):
+            bins = x_part[0, c, band * BINS : (band + 1) * BINS, :]
+            nc.sync.dma_start(
+                out=raw[:, r, c, :, :].rearrange("p (g u) t -> p g (u t)", u=2),
+                in_=bins.rearrange("(g p u) t -> p g (u t)", p=P, u=2),
+            )
+    return raw
+
+
+def load_words(nc, pool, fc_w_words, k):
+    words = pool.tile([P, EMB], U32, tag="words", name="words%d" % k, align_bytes=64)
+    nc.sync.dma_start(out=words[:].bitcast(I32), in_=fc_w_words[k].rearrange("p n t -> p (n t)").bitcast(I32))
+    return words
+
+
+def statistics(nc, ln, stat_pool, band, raw, ones_bf, ident_bf, ident_f32):
+    chunks = [raw[:, r, c, :, :] for r in range(PARTS) for c in range(CHANNELS)]
+
+    mean_ps = stat_pool.tile([P, 2 * FRAMES], F32, tag="stat", name="mean_ps%d" % band)
+    feature_sum = mean_ps[:, FRAMES : FRAMES + 1]
+    for i, chunk in enumerate(chunks):
+        for s in range(SLICES_C):
+            nc.tensor.matmul(
+                out=feature_sum,
+                lhsT=chunk[:, s, :],
+                rhs=ones_bf,
+                start=(i == 0 and s == 0),
+                stop=(i == len(chunks) - 1 and s == SLICES_C - 1),
+            )
+    neg_mean = ln.tile([P, 1], F32, tag="neg_mean")
+    nc.vector.tensor_scalar_mul(out=neg_mean[:], in0=feature_sum, scalar1=-1.0 / FEAT)
+    spread_over_partitions(nc, mean_ps[:, 0:FRAMES], neg_mean[:], ident_f32)
+    neg_mean_row = ln.tile([P, FRAMES], F32, tag="neg_mean_row")
+    nc.scalar.copy(out=neg_mean_row[:], in_=mean_ps[:, 0:FRAMES])
+
+    square_sums = ln.tile([P, len(chunks)], F32, tag="square_sums")
+    for i, chunk in enumerate(chunks):
+        frames_first = stat_pool.tile([P, SLICES_C, P], BF16, tag="stat")
+        for s in range(SLICES_C):
+            nc.tensor.transpose(out=frames_first[:, s, :], in_=chunk[:, s, :], identity=ident_bf)
+        squares = ln.tile([P, SLICES_C * P], BF16, tag="squares")
+        nc.scalar.activation(
+            out=squares[:],
+            in_=frames_first[:].rearrange("t s k -> t (s k)"),
+            func=ACT.Square,
+            bias=neg_mean[:],
+            accum_out=square_sums[:, i : i + 1],
+        )
+    square_sum = ln.tile([P, 1], F32, tag="square_sum")
+    nc.vector.tensor_reduce(out=square_sum[:], in_=square_sums[:], axis=mybir.AxisListType.X, op=ALU.add)
+    var_eps = ln.tile([P, 1], F32, tag="var_eps")
+    nc.vector.tensor_scalar(
+        out=var_eps[:], in0=square_sum[:], scalar1=1.0 / FEAT, scalar2=EPS, op0=ALU.mult, op1=ALU.add
+    )
+    inverse = ln.tile([P, 1], F32, tag="inverse")
+    nc.vector.reciprocal(out=inverse[:], in_=var_eps[:])
+    inverse_ps = stat_pool.tile([P, FRAMES], F32, tag="stat", name="inverse_ps%d" % band)
+    spread_over_partitions(nc, inverse_ps[:], inverse[:], ident_f32)
+    rstd_row = ln.tile([P, FRAMES], F32, tag="rstd_row")
+    nc.scalar.sqrt(out=rstd_row[:], in_=inverse_ps[:])
+    return neg_mean_row, rstd_row
+
+
+def normalise_and_quantise(nc, ln, band, c, raw, neg_mean_row, rstd_row, params, codes, code_scales):
+    scaled = ln.tile([P, PARTS, SLICES_C, FRAMES], F32, tag="scaled", bufs=BANDS * CHANNELS)
+    for r in range(PARTS):
+        nc.vector.tensor_tensor(
+            out=scaled[:, r, :, :],
+            in0=raw[:, r, c, :, :],
+            in1=neg_mean_row[:].unsqueeze(1).to_broadcast([P, SLICES_C, FRAMES]),
+            op=ALU.add,
+        )
+    for r in range(PARTS):
+        nc.vector.tensor_tensor(
+            out=scaled[:, r, :, :],
+            in0=scaled[:, r, :, :],
+            in1=rstd_row[:].unsqueeze(1).to_broadcast([P, SLICES_C, FRAMES]),
+            op=ALU.mult,
+        )
+    xn = ln.tile([P, GROUPS_C, PACK, FRAMES], BF16, tag="xn")
+    for r in range(PARTS):
+        for g in range(GROUPS_C):
+            for u in range(2):
+                j = 2 * u + r
+                row = band * GROUPS + c * GROUPS_C + g
+                gain = params[:, j, GAIN_ROW + row : GAIN_ROW + row + 1]
+                shift = params[:, j, SHIFT_ROW + row : SHIFT_ROW + row + 1]
+                if u == 0:
+                    nc.scalar.activation(
+                        out=xn[:, g, j, :], in_=scaled[:, r, 2 * g + u, :], func=ACT.Identity, scale=gain, bias=shift
+                    )
+                else:
+                    nc.vector.tensor_scalar(
+                        out=xn[:, g, j, :],
+                        in0=scaled[:, r, 2 * g + u, :],
+                        scalar1=gain,
+                        scalar2=shift,
+                        op0=ALU.mult,
+                        op1=ALU.add,
+                    )
+    grouped = ln.tile([P, GROUPS_C, FRAMES, PACK], BF16, tag="grouped", align_bytes=64)
+    nc.vector.tensor_copy(out=grouped[:], in_=xn[:].rearrange("p g j t -> p g t j"))
+    columns = slice(c * GROUPS_C * FRAMES, (c + 1) * GROUPS_C * FRAMES)
+    nc.vector.quantize_mx(
+        out=codes[:, columns].bitcast(FP8X4),
+        scales=code_scales[:, columns],
+        in_=grouped[:].rearrange("p g t j -> p (g t j)"),
+    )
+
+
+def tile_bandsplitmodule_w_e_kernel(tc, x_real, x_imag, ln_w, ln_b, fc_w_words, fc_w_scales, fc_b, out):
+    nc = tc.nc
+    with ExitStack() as stack:
+        const = stack.enter_context(tc.tile_pool(name="const", bufs=1))
+        weights = stack.enter_context(tc.tile_pool(name="weights", bufs=W_BUFS))
+        acc_pool = stack.enter_context(tc.psum_pool(name="acc", bufs=N_TILES))
+        stat_pool = stack.enter_context(tc.psum_pool(name="stat", bufs=2))
+
+        small = const.tile([P, K_PASS], BF16)
+        nc.vector.memset(small[:], 0.0)
+        nc.scalar.dma_start(
+            out=small[GAIN_ROW : GAIN_ROW + BANDS * GROUPS, :], in_=ln_w.rearrange("n (g k) -> (n g) k", k=K_PASS)
+        )
+        nc.scalar.dma_start(
+            out=small[SHIFT_ROW : SHIFT_ROW + BANDS * GROUPS, :], in_=ln_b.rearrange("n (g k) -> (n g) k", k=K_PASS)
+        )
+        nc.scalar.dma_start(
+            out=small[FC_B_ROW : FC_B_ROW + BANDS * N_TILES, :], in_=fc_b.rearrange("n (c e) -> (n c) e", e=N_TILE)
+        )
+
+        ident_bf = const.tile([P, P], BF16)
+        make_identity(nc, ident_bf[:])
+        ident_f32 = const.tile([P, P], F32)
+        make_identity(nc, ident_f32[:])
+        ones_bf = const.tile([P, 1], BF16)
+        nc.vector.memset(ones_bf[:], 1.0)
+        ones_f32 = const.tile([P, 1], F32)
+        nc.vector.memset(ones_f32[:], 1.0)
+
+        first_table = const.tile([P, 1], F32)
+        nc.scalar.sqrt(out=first_table[:], in_=ones_f32[:])
+
+        with tc.tile_pool(name="ln", bufs=BANDS) as ln:
+            raw = [load_band(nc, ln, x_real, x_imag, band) for band in range(BANDS)]
+            words = [load_words(nc, weights, fc_w_words, k) for k in range(W_BUFS)]
+
+            planes = const.tile([P, PLANES, EMB], U8, align_bytes=64)
+            nc.vector.memset(planes[:].rearrange("p a n -> p (a n)").bitcast(I32), 0)
+            for a in range(BANDS * GROUPS // PLANES):
+                for quadrant in range(QUADRANTS):
+                    nc.gpsimd.dma_start(
+                        out=planes[32 * quadrant : 32 * quadrant + 4 * PLANES, a, :].bitcast(F32),
+                        in_=fc_w_scales[PLANES * a : PLANES * (a + 1), 4 * quadrant : 4 * (quadrant + 1), :].bitcast(F32),
+                    )
+
+            params_ps = stat_pool.tile([P, PACK, P], BF16, tag="stat")
+            for j in range(PACK):
+                nc.tensor.transpose(out=params_ps[:, j, :], in_=small[:, j:K_PASS:PACK], identity=ident_bf[:])
+            params = const.tile([P, PACK, FC_B_ROW], F32)
+            nc.vector.tensor_copy(out=params[:], in_=params_ps[:, :, 0:FC_B_ROW])
+
+            bias = const.tile([P, BANDS * EMB], BF16)
+            for i in range(BANDS * N_TILES // 2):
+                bias_ps = stat_pool.tile([P, 2, N_TILE], BF16, tag="stat")
+                for h in range(2):
+                    row = FC_B_ROW + 2 * i + h
+                    nc.tensor.matmul(
+                        out=bias_ps[:, h, :],
+                        lhsT=ident_bf[:, row : row + 1].to_broadcast([P, P]),
+                        rhs=small[:],
+                        start=True,
+                        stop=True,
+                    )
+                nc.scalar.copy(
+                    out=bias[:, 2 * i * N_TILE : 2 * (i + 1) * N_TILE], in_=bias_ps[:].rearrange("p h n -> p (h n)")
+                )
+
+            rows = [
+                statistics(nc, ln, stat_pool, band, raw[band], ones_bf[:], ident_bf[:], ident_f32[:])
+                for band in range(BANDS)
+            ]
+            codes = [const.tile([P, GROUPS * FRAMES], U32, name="codes%d" % band, align_bytes=64) for band in range(BANDS)]
+            code_scales = [
+                const.tile([P, GROUPS * FRAMES], U8, name="code_scales%d" % band, align_bytes=64) for band in range(BANDS)
+            ]
+            for band in range(BANDS):
+                for c in range(CHANNELS):
+                    normalise_and_quantise(nc, ln, band, c, raw[band], *rows[band], params, codes[band], code_scales[band])
+
+        results = stack.enter_context(tc.tile_pool(name="results", bufs=BANDS))
+        for band in range(BANDS):
+            acc = [acc_pool.tile([P, N_TILE], F32, tag="acc", name="acc%d_%d" % (band, n)) for n in range(N_TILES)]
+            for g in range(GROUPS):
+                k = band * GROUPS + g
+                a, b = divmod(k, PLANES)
+                frames = slice(g * FRAMES, (g + 1) * FRAMES)
+                for n in range(N_TILES):
+                    cols = slice(n * N_TILE, (n + 1) * N_TILE)
+                    nc.tensor.matmul_mx(
+                        out=acc[n][:],
+                        lhsT=codes[band][:, frames].bitcast(FP8X4),
+                        lhsT_scale=code_scales[band][:, frames],
+                        rhs=words[k][:, cols].bitcast(FP8X4),
+                        rhs_scale=planes[4 * b : P, a, cols],
+                        start=(g == 0),
+                        stop=(g == GROUPS - 1),
+                    )
+                if k + W_BUFS < BANDS * GROUPS:
+                    words.append(load_words(nc, weights, fc_w_words, k + W_BUFS))
+            result = results.tile([P, EMB], F32, tag="result")
+            for n in range(N_TILES):
+                cols = slice(n * N_TILE, (n + 1) * N_TILE)
+                bias_cols = slice(band * EMB + n * N_TILE, band * EMB + (n + 1) * N_TILE)
+                nc.vector.tensor_tensor(out=result[:, cols], in0=acc[n][:], in1=bias[:, bias_cols], op=ALU.add)
+                if n % STORE_TILES == STORE_TILES - 1:
+                    stored = slice((n + 1 - STORE_TILES) * N_TILE, (n + 1) * N_TILE)
+                    nc.sync.dma_start(out=out[0, band, :, stored], in_=result[:, stored])

@@ -25,7 +25,8 @@ EMB = 3072
 EPS = 1e-5
 GROUPS = FEAT // K_PASS
 GROUPS_C = GROUPS // CHANNELS
-SLICES_C = 2 * GROUPS_C
+RUNS = BANDS * GROUPS_C
+ROW_BINS = BANDS * BINS // P
 N_TILE = 512
 N_TILES = EMB // N_TILE
 PLANES = 4
@@ -40,115 +41,66 @@ FC_B_ROW = 2 * BANDS * GROUPS
 FLOPS = 2 * BANDS * FRAMES * FEAT * EMB
 
 
-def spread_over_partitions(nc, row, column, ident):
-    nc.tensor.matmul(out=row, lhsT=column.to_broadcast([P, P]), rhs=ident, start=True, stop=True)
-
-
-def load_band(nc, pool, x_real, x_imag, band):
-    raw = pool.tile([P, PARTS, CHANNELS, SLICES_C, FRAMES], BF16, tag="raw", name="raw%d" % band)
-    for r, x_part in enumerate((x_real, x_imag)):
-        for c in range(CHANNELS):
-            bins = x_part[0, c, band * BINS : (band + 1) * BINS, :]
-            nc.sync.dma_start(
-                out=raw[:, r, c, :, :].rearrange("p (g u) t -> p g (u t)", u=2),
-                in_=bins.rearrange("(g p u) t -> p g (u t)", p=P, u=2),
-            )
-    return raw
-
-
 def load_words(nc, pool, fc_w_words, k):
     words = pool.tile([P, EMB], U32, tag="words", name="words%d" % k, align_bytes=64)
     nc.sync.dma_start(out=words[:].bitcast(I32), in_=fc_w_words[k].rearrange("p n t -> p (n t)").bitcast(I32))
     return words
 
 
-def statistics(nc, ln, stat_pool, band, raw, ones_bf, ident_bf, ident_f32):
-    chunks = [raw[:, r, c, :, :] for r in range(PARTS) for c in range(CHANNELS)]
-
-    mean_ps = stat_pool.tile([P, 2 * FRAMES], F32, tag="stat", name="mean_ps%d" % band)
-    feature_sum = mean_ps[:, FRAMES : FRAMES + 1]
-    for i, chunk in enumerate(chunks):
-        for s in range(SLICES_C):
-            nc.tensor.matmul(
-                out=feature_sum,
-                lhsT=chunk[:, s, :],
-                rhs=ones_bf,
-                start=(i == 0 and s == 0),
-                stop=(i == len(chunks) - 1 and s == SLICES_C - 1),
-            )
-    neg_mean = ln.tile([P, 1], F32, tag="neg_mean")
-    nc.vector.tensor_scalar_mul(out=neg_mean[:], in0=feature_sum, scalar1=-1.0 / FEAT)
-    spread_over_partitions(nc, mean_ps[:, 0:FRAMES], neg_mean[:], ident_f32)
-    neg_mean_row = ln.tile([P, FRAMES], F32, tag="neg_mean_row")
-    nc.scalar.copy(out=neg_mean_row[:], in_=mean_ps[:, 0:FRAMES])
-
-    square_sums = ln.tile([P, len(chunks)], F32, tag="square_sums")
-    for i, chunk in enumerate(chunks):
-        frames_first = stat_pool.tile([P, SLICES_C, P], BF16, tag="stat")
-        for s in range(SLICES_C):
-            nc.tensor.transpose(out=frames_first[:, s, :], in_=chunk[:, s, :], identity=ident_bf)
-        squares = ln.tile([P, SLICES_C * P], BF16, tag="squares")
-        nc.scalar.activation(
-            out=squares[:],
-            in_=frames_first[:].rearrange("t s k -> t (s k)"),
-            func=ACT.Square,
-            bias=neg_mean[:],
-            accum_out=square_sums[:, i : i + 1],
-        )
-    square_sum = ln.tile([P, 1], F32, tag="square_sum")
-    nc.vector.tensor_reduce(out=square_sum[:], in_=square_sums[:], axis=mybir.AxisListType.X, op=ALU.add)
-    var_eps = ln.tile([P, 1], F32, tag="var_eps")
-    nc.vector.tensor_scalar(
-        out=var_eps[:], in0=square_sum[:], scalar1=1.0 / FEAT, scalar2=EPS, op0=ALU.mult, op1=ALU.add
-    )
-    inverse = ln.tile([P, 1], F32, tag="inverse")
-    nc.vector.reciprocal(out=inverse[:], in_=var_eps[:])
-    inverse_ps = stat_pool.tile([P, FRAMES], F32, tag="stat", name="inverse_ps%d" % band)
-    spread_over_partitions(nc, inverse_ps[:], inverse[:], ident_f32)
-    rstd_row = ln.tile([P, FRAMES], F32, tag="rstd_row")
-    nc.scalar.sqrt(out=rstd_row[:], in_=inverse_ps[:])
-    return neg_mean_row, rstd_row
-
-
-def normalise_and_quantise(nc, ln, band, c, raw, neg_mean_row, rstd_row, params, codes, code_scales):
-    scaled = ln.tile([P, PARTS, SLICES_C, FRAMES], F32, tag="scaled", bufs=BANDS * CHANNELS)
-    for r in range(PARTS):
-        nc.vector.tensor_tensor(
-            out=scaled[:, r, :, :],
-            in0=raw[:, r, c, :, :],
-            in1=neg_mean_row[:].unsqueeze(1).to_broadcast([P, SLICES_C, FRAMES]),
-            op=ALU.add,
-        )
-    for r in range(PARTS):
-        nc.vector.tensor_tensor(
-            out=scaled[:, r, :, :],
-            in0=scaled[:, r, :, :],
-            in1=rstd_row[:].unsqueeze(1).to_broadcast([P, SLICES_C, FRAMES]),
-            op=ALU.mult,
-        )
-    xn = ln.tile([P, GROUPS_C, PACK, FRAMES], BF16, tag="xn")
-    for r in range(PARTS):
-        for g in range(GROUPS_C):
+def to_frames_first(nc, ln, acc_pool, x_rows, xt, sums, ident_bf):
+    i = 0
+    for c in range(CHANNELS):
+        for r in range(PARTS):
             for u in range(2):
-                j = 2 * u + r
-                row = band * GROUPS + c * GROUPS_C + g
-                gain = params[:, j, GAIN_ROW + row : GAIN_ROW + row + 1]
-                shift = params[:, j, SHIFT_ROW + row : SHIFT_ROW + row + 1]
-                if u == 0:
-                    nc.scalar.activation(
-                        out=xn[:, g, j, :], in_=scaled[:, r, 2 * g + u, :], func=ACT.Identity, scale=gain, bias=shift
-                    )
-                else:
-                    nc.vector.tensor_scalar(
-                        out=xn[:, g, j, :],
-                        in0=scaled[:, r, 2 * g + u, :],
-                        scalar1=gain,
-                        scalar2=shift,
-                        op0=ALU.mult,
-                        op1=ALU.add,
-                    )
+                turned = acc_pool.tile([P, ROW_BINS // 2, P], BF16, tag="acc")
+                for b in range(ROW_BINS // 2):
+                    nc.tensor.transpose(out=turned[:, b, :], in_=x_rows[r][c][:, 2 * b + u, :], identity=ident_bf)
+                nc.scalar.copy(
+                    out=xt[:, :, c, u, r, :].rearrange("t n (i b) -> t n i b", b=ROW_BINS // 2),
+                    in_=turned[:].rearrange("t b (n i) -> t n i b", n=RUNS),
+                )
+                for band in range(BANDS):
+                    half = slice(band * P // BANDS, (band + 1) * P // BANDS)
+                    nc.vector.bn_stats(out=sums[:, band, i, :], in_=turned[:, :, half])
+                i += 1
+
+
+def normalise(nc, ln, band, c, xt, stats, rstd):
+    y = ln.tile([P, GROUPS_C, PACK, P], F32, tag="y")
+    nc.vector.tensor_scalar(
+        out=y[:].rearrange("t g j p -> t g (j p)"),
+        in0=xt[:, band * GROUPS_C : (band + 1) * GROUPS_C, c, :, :, :].rearrange("t g u r p -> t g (u r p)"),
+        scalar1=stats[:, band, 0:1],
+        scalar2=rstd[:, band : band + 1],
+        op0=ALU.subtract,
+        op1=ALU.mult,
+    )
+    return y
+
+
+def back_to_features_first(nc, pool, tag, band, c, g, y, xn, params, ident_f32):
+    back = pool.tile([P, PACK, FRAMES], F32, tag=tag)
+    for j in range(PACK):
+        nc.tensor.transpose(out=back[:, j, :], in_=y[:, g, j, :], identity=ident_f32)
+    row = band * GROUPS + c * GROUPS_C + g
+    for j in range(PACK):
+        gain = params[:, j, GAIN_ROW + row : GAIN_ROW + row + 1]
+        shift = params[:, j, SHIFT_ROW + row : SHIFT_ROW + row + 1]
+        if g % 2 == 0:
+            nc.scalar.activation(out=xn[:, g, j, :], in_=back[:, j, :], func=ACT.Identity, scale=gain, bias=shift)
+        else:
+            nc.vector.tensor_scalar(
+                out=xn[:, g, j, :], in0=back[:, j, :], scalar1=gain, scalar2=shift, op0=ALU.mult, op1=ALU.add
+            )
+
+
+def interleave(nc, ln, xn):
     grouped = ln.tile([P, GROUPS_C, FRAMES, PACK], BF16, tag="grouped", align_bytes=64)
     nc.vector.tensor_copy(out=grouped[:], in_=xn[:].rearrange("p g j t -> p g t j"))
+    return grouped
+
+
+def quantise(nc, c, grouped, codes, code_scales):
     columns = slice(c * GROUPS_C * FRAMES, (c + 1) * GROUPS_C * FRAMES)
     nc.vector.quantize_mx(
         out=codes[:, columns].bitcast(FP8X4),
@@ -157,13 +109,42 @@ def normalise_and_quantise(nc, ln, band, c, raw, neg_mean_row, rstd_row, params,
     )
 
 
+def spread_bias(nc, stat_pool, small, ident_bf, bias, i):
+    bias_ps = stat_pool.tile([P, 2, N_TILE], BF16, tag="stat")
+    for h in range(2):
+        row = FC_B_ROW + 2 * i + h
+        nc.tensor.matmul(
+            out=bias_ps[:, h, :],
+            lhsT=ident_bf[:, row : row + 1].to_broadcast([P, P]),
+            rhs=small[:],
+            start=True,
+            stop=True,
+        )
+    nc.scalar.copy(out=bias[:, 2 * i * N_TILE : 2 * (i + 1) * N_TILE], in_=bias_ps[:].rearrange("p h n -> p (h n)"))
+
+
 def tile_bandsplitmodule_w_e_kernel(tc, x_real, x_imag, ln_w, ln_b, fc_w_words, fc_w_scales, fc_b, out):
     nc = tc.nc
     with ExitStack() as stack:
         const = stack.enter_context(tc.tile_pool(name="const", bufs=1))
         weights = stack.enter_context(tc.tile_pool(name="weights", bufs=W_BUFS))
+        results = stack.enter_context(tc.tile_pool(name="results", bufs=3))
+        ln = stack.enter_context(tc.tile_pool(name="ln", bufs=2))
         acc_pool = stack.enter_context(tc.psum_pool(name="acc", bufs=N_TILES))
         stat_pool = stack.enter_context(tc.psum_pool(name="stat", bufs=2))
+        stack.enter_context(tc.manual_schedule())
+
+        x_rows = [
+            [const.tile([P, ROW_BINS, FRAMES], BF16, name="x_rows%d%d" % (r, c)) for c in range(CHANNELS)]
+            for r in range(PARTS)
+        ]
+        for c in range(CHANNELS):
+            for r, x_part in enumerate((x_real, x_imag)):
+                nc.sync.dma_start(
+                    out=x_rows[r][c][:].rearrange("q b t -> q (b t)"),
+                    in_=x_part[0, c].rearrange("(q b) t -> q (b t)", b=ROW_BINS),
+                )
+        words = [load_words(nc, weights, fc_w_words, k) for k in range(W_BUFS)]
 
         small = const.tile([P, K_PASS], BF16)
         nc.vector.memset(small[:], 0.0)
@@ -181,65 +162,80 @@ def tile_bandsplitmodule_w_e_kernel(tc, x_real, x_imag, ln_w, ln_b, fc_w_words, 
         make_identity(nc, ident_bf[:])
         ident_f32 = const.tile([P, P], F32)
         make_identity(nc, ident_f32[:])
-        ones_bf = const.tile([P, 1], BF16)
-        nc.vector.memset(ones_bf[:], 1.0)
         ones_f32 = const.tile([P, 1], F32)
         nc.vector.memset(ones_f32[:], 1.0)
 
         first_table = const.tile([P, 1], F32)
         nc.scalar.sqrt(out=first_table[:], in_=ones_f32[:])
 
-        with tc.tile_pool(name="ln", bufs=BANDS) as ln:
-            raw = [load_band(nc, ln, x_real, x_imag, band) for band in range(BANDS)]
-            words = [load_words(nc, weights, fc_w_words, k) for k in range(W_BUFS)]
-
-            planes = const.tile([P, PLANES, EMB], U8, align_bytes=64)
-            nc.vector.memset(planes[:].rearrange("p a n -> p (a n)").bitcast(I32), 0)
-            for a in range(BANDS * GROUPS // PLANES):
-                for quadrant in range(QUADRANTS):
-                    nc.gpsimd.dma_start(
-                        out=planes[32 * quadrant : 32 * quadrant + 4 * PLANES, a, :].bitcast(F32),
-                        in_=fc_w_scales[PLANES * a : PLANES * (a + 1), 4 * quadrant : 4 * (quadrant + 1), :].bitcast(F32),
-                    )
-
-            params_ps = stat_pool.tile([P, PACK, P], BF16, tag="stat")
-            for j in range(PACK):
-                nc.tensor.transpose(out=params_ps[:, j, :], in_=small[:, j:K_PASS:PACK], identity=ident_bf[:])
-            params = const.tile([P, PACK, FC_B_ROW], F32)
-            nc.vector.tensor_copy(out=params[:], in_=params_ps[:, :, 0:FC_B_ROW])
-
-            bias = const.tile([P, BANDS * EMB], BF16)
-            for i in range(BANDS * N_TILES // 2):
-                bias_ps = stat_pool.tile([P, 2, N_TILE], BF16, tag="stat")
-                for h in range(2):
-                    row = FC_B_ROW + 2 * i + h
-                    nc.tensor.matmul(
-                        out=bias_ps[:, h, :],
-                        lhsT=ident_bf[:, row : row + 1].to_broadcast([P, P]),
-                        rhs=small[:],
-                        start=True,
-                        stop=True,
-                    )
-                nc.scalar.copy(
-                    out=bias[:, 2 * i * N_TILE : 2 * (i + 1) * N_TILE], in_=bias_ps[:].rearrange("p h n -> p (h n)")
+        planes = const.tile([P, PLANES, EMB], U8, align_bytes=64)
+        nc.vector.memset(planes[:].rearrange("p a n -> p (a n)").bitcast(I32), 0)
+        for a in range(BANDS * GROUPS // PLANES):
+            for quadrant in range(QUADRANTS):
+                nc.gpsimd.dma_start(
+                    out=planes[32 * quadrant : 32 * quadrant + 4 * PLANES, a, :].bitcast(F32),
+                    in_=fc_w_scales[PLANES * a : PLANES * (a + 1), 4 * quadrant : 4 * (quadrant + 1), :].bitcast(F32),
                 )
 
-            rows = [
-                statistics(nc, ln, stat_pool, band, raw[band], ones_bf[:], ident_bf[:], ident_f32[:])
-                for band in range(BANDS)
-            ]
-            codes = [const.tile([P, GROUPS * FRAMES], U32, name="codes%d" % band, align_bytes=64) for band in range(BANDS)]
-            code_scales = [
-                const.tile([P, GROUPS * FRAMES], U8, name="code_scales%d" % band, align_bytes=64) for band in range(BANDS)
-            ]
-            for band in range(BANDS):
-                for c in range(CHANNELS):
-                    normalise_and_quantise(nc, ln, band, c, raw[band], *rows[band], params, codes[band], code_scales[band])
+        xt = const.tile([P, RUNS, CHANNELS, 2, PARTS, P], BF16)
+        sums = const.tile([P, BANDS, CHANNELS * PARTS * 2, 6], F32)
+        to_frames_first(nc, ln, acc_pool, x_rows, xt, sums, ident_bf[:])
 
-        results = stack.enter_context(tc.tile_pool(name="results", bufs=BANDS))
+        params_ps = stat_pool.tile([P, PACK, P], BF16, tag="stat")
+        for j in range(PACK):
+            nc.tensor.transpose(out=params_ps[:, j, :], in_=small[:, j:K_PASS:PACK], identity=ident_bf[:])
+        params = const.tile([P, PACK, FC_B_ROW], F32)
+        nc.scalar.copy(out=params[:], in_=params_ps[:, :, 0:FC_B_ROW])
+
+        stats = const.tile([P, BANDS, 2], F32)
+        for band in range(BANDS):
+            nc.vector.bn_aggr(out=stats[:, band, :], in_=sums[:, band, :, :].rearrange("t i s -> t (i s)"))
+        var_eps = const.tile([P, BANDS], F32)
+        nc.vector.tensor_scalar_add(out=var_eps[:], in0=stats[:, :, 1], scalar1=EPS)
+        inverse = const.tile([P, BANDS], F32)
+        nc.vector.reciprocal(out=inverse[:], in_=var_eps[:])
+        rstd = const.tile([P, BANDS], F32)
+        nc.scalar.sqrt(out=rstd[:], in_=inverse[:])
+
+        bias = const.tile([P, BANDS * EMB], BF16)
+
+        codes = [const.tile([P, GROUPS * FRAMES], U32, name="codes%d" % band, align_bytes=64) for band in range(BANDS)]
+        code_scales = [
+            const.tile([P, GROUPS * FRAMES], U8, name="code_scales%d" % band, align_bytes=64) for band in range(BANDS)
+        ]
+
+        steps = [(band, c) for band in range(BANDS) for c in range(CHANNELS)]
+        ys = {}
+        xns = {}
+
+        def turn_back(i):
+            band, c = steps[i]
+            xns[i] = ln.tile([P, GROUPS_C, PACK, FRAMES], BF16, tag="xn", name="xn%d" % i)
+            pool, tag = (acc_pool, "acc") if band == 0 else (stat_pool, "stat")
+            for g in range(GROUPS_C):
+                back_to_features_first(nc, pool, tag, band, c, g, ys[i], xns[i], params, ident_f32[:])
+
+        def finish(i):
+            band, c = steps[i]
+            grouped = interleave(nc, ln, xns[i])
+            if i + 2 < len(steps):
+                ys[i + 2] = normalise(nc, ln, *steps[i + 2], xt, stats, rstd)
+            quantise(nc, c, grouped, codes[band], code_scales[band])
+
+        for i in range(2):
+            ys[i] = normalise(nc, ln, *steps[i], xt, stats, rstd)
+        for i in range(3):
+            turn_back(i)
+            finish(i)
+
         for band in range(BANDS):
             acc = [acc_pool.tile([P, N_TILE], F32, tag="acc", name="acc%d_%d" % (band, n)) for n in range(N_TILES)]
             for g in range(GROUPS):
+                if band == 0 and g == 2:
+                    turn_back(3)
+                    finish(3)
+                if band == 0 and g >= 2:
+                    spread_bias(nc, stat_pool, small, ident_bf, bias, g - 2)
                 k = band * GROUPS + g
                 a, b = divmod(k, PLANES)
                 frames = slice(g * FRAMES, (g + 1) * FRAMES)
@@ -256,11 +252,13 @@ def tile_bandsplitmodule_w_e_kernel(tc, x_real, x_imag, ln_w, ln_b, fc_w_words, 
                     )
                 if k + W_BUFS < BANDS * GROUPS:
                     words.append(load_words(nc, weights, fc_w_words, k + W_BUFS))
-            result = results.tile([P, EMB], F32, tag="result")
-            for n in range(N_TILES):
-                cols = slice(n * N_TILE, (n + 1) * N_TILE)
-                bias_cols = slice(band * EMB + n * N_TILE, band * EMB + (n + 1) * N_TILE)
-                nc.vector.tensor_tensor(out=result[:, cols], in0=acc[n][:], in1=bias[:, bias_cols], op=ALU.add)
-                if n % STORE_TILES == STORE_TILES - 1:
-                    stored = slice((n + 1 - STORE_TILES) * N_TILE, (n + 1) * N_TILE)
-                    nc.sync.dma_start(out=out[0, band, :, stored], in_=result[:, stored])
+            for m in range(N_TILES // STORE_TILES):
+                result = results.tile([P, STORE_TILES * N_TILE], F32, tag="result")
+                for h in range(STORE_TILES):
+                    n = m * STORE_TILES + h
+                    bias_cols = slice(band * EMB + n * N_TILE, band * EMB + (n + 1) * N_TILE)
+                    nc.vector.tensor_tensor(
+                        out=result[:, h * N_TILE : (h + 1) * N_TILE], in0=acc[n][:], in1=bias[:, bias_cols], op=ALU.add
+                    )
+                stored = slice(m * STORE_TILES * N_TILE, (m + 1) * STORE_TILES * N_TILE)
+                nc.sync.dma_start(out=out[0, band, :, stored], in_=result[:])

@@ -31,8 +31,8 @@ N_TILE = 512
 N_TILES = EMB // N_TILE
 PLANES = 4
 QUADRANTS = 4
-W_BUFS = 10
-STORE_TILES = 2
+W_PAIRS = 5
+STORE_TILES = (3, 2)
 
 GAIN_ROW = 0
 SHIFT_ROW = BANDS * GROUPS
@@ -41,20 +41,24 @@ FC_B_ROW = 2 * BANDS * GROUPS
 FLOPS = 2 * BANDS * FRAMES * FEAT * EMB
 
 
-def load_words(nc, pool, fc_w_words, k):
-    words = pool.tile([P, EMB], U32, tag="words", name="words%d" % k, align_bytes=64)
-    nc.sync.dma_start(out=words[:].bitcast(I32), in_=fc_w_words[k].rearrange("p n t -> p (n t)").bitcast(I32))
+def load_words(nc, pool, fc_w_words, k, singly=False):
+    words = pool.tile([P, 2, EMB], U32, tag="words", name="words%d" % k, align_bytes=64)
+    for first, count in ((0, 1), (1, 1)) if singly else ((0, 2),):
+        nc.sync.dma_start(
+            out=words[:, first : first + count, :].bitcast(I32),
+            in_=fc_w_words[k + first : k + first + count].rearrange("g p n t -> p g (n t)").bitcast(I32),
+        )
     return words
 
 
 def to_frames_first(nc, ln, acc_pool, x_rows, xt, sums, ident_bf):
     i = 0
-    for c in range(CHANNELS):
-        for r in range(PARTS):
+    for r in range(PARTS):
+        for c in range(CHANNELS):
             for u in range(2):
                 turned = acc_pool.tile([P, ROW_BINS // 2, P], BF16, tag="acc")
                 for b in range(ROW_BINS // 2):
-                    nc.tensor.transpose(out=turned[:, b, :], in_=x_rows[r][c][:, 2 * b + u, :], identity=ident_bf)
+                    nc.tensor.transpose(out=turned[:, b, :], in_=x_rows[r][:, c, 2 * b + u, :], identity=ident_bf)
                 nc.scalar.copy(
                     out=xt[:, :, c, u, r, :].rearrange("t n (i b) -> t n i b", b=ROW_BINS // 2),
                     in_=turned[:].rearrange("t b (n i) -> t n i b", n=RUNS),
@@ -127,24 +131,21 @@ def tile_bandsplitmodule_w_e_kernel(tc, x_real, x_imag, ln_w, ln_b, fc_w_words, 
     nc = tc.nc
     with ExitStack() as stack:
         const = stack.enter_context(tc.tile_pool(name="const", bufs=1))
-        weights = stack.enter_context(tc.tile_pool(name="weights", bufs=W_BUFS))
-        results = stack.enter_context(tc.tile_pool(name="results", bufs=3))
+        weights = stack.enter_context(tc.tile_pool(name="weights", bufs=W_PAIRS))
+        io = stack.enter_context(tc.tile_pool(name="io", bufs=4))
         ln = stack.enter_context(tc.tile_pool(name="ln", bufs=2))
         acc_pool = stack.enter_context(tc.psum_pool(name="acc", bufs=N_TILES))
         stat_pool = stack.enter_context(tc.psum_pool(name="stat", bufs=2))
         stack.enter_context(tc.manual_schedule())
 
-        x_rows = [
-            [const.tile([P, ROW_BINS, FRAMES], BF16, name="x_rows%d%d" % (r, c)) for c in range(CHANNELS)]
-            for r in range(PARTS)
-        ]
-        for c in range(CHANNELS):
-            for r, x_part in enumerate((x_real, x_imag)):
-                nc.sync.dma_start(
-                    out=x_rows[r][c][:].rearrange("q b t -> q (b t)"),
-                    in_=x_part[0, c].rearrange("(q b) t -> q (b t)", b=ROW_BINS),
-                )
-        words = [load_words(nc, weights, fc_w_words, k) for k in range(W_BUFS)]
+        x_rows = []
+        for r, x_part in enumerate((x_real, x_imag)):
+            x_rows.append(io.tile([P, CHANNELS, ROW_BINS, FRAMES], BF16, tag="io", name="x_rows%d" % r))
+            nc.sync.dma_start(
+                out=x_rows[r][:].rearrange("q c b t -> q c (b t)"),
+                in_=x_part[0].rearrange("c (q b) t -> q c (b t)", b=ROW_BINS),
+            )
+        words = [load_words(nc, weights, fc_w_words, 2 * i) for i in range(W_PAIRS)]
 
         small = const.tile([P, K_PASS], BF16)
         nc.vector.memset(small[:], 0.0)
@@ -245,20 +246,23 @@ def tile_bandsplitmodule_w_e_kernel(tc, x_real, x_imag, ln_w, ln_b, fc_w_words, 
                         out=acc[n][:],
                         lhsT=codes[band][:, frames].bitcast(FP8X4),
                         lhsT_scale=code_scales[band][:, frames],
-                        rhs=words[k][:, cols].bitcast(FP8X4),
+                        rhs=words[k // 2][:, k % 2, cols].bitcast(FP8X4),
                         rhs_scale=planes[4 * b : P, a, cols],
                         start=(g == 0),
                         stop=(g == GROUPS - 1),
                     )
-                if k + W_BUFS < BANDS * GROUPS:
-                    words.append(load_words(nc, weights, fc_w_words, k + W_BUFS))
-            for m in range(N_TILES // STORE_TILES):
-                result = results.tile([P, STORE_TILES * N_TILE], F32, tag="result")
-                for h in range(STORE_TILES):
-                    n = m * STORE_TILES + h
+                if k % 2 == 1 and k + 2 * W_PAIRS < BANDS * GROUPS:
+                    next_pair = k - 1 + 2 * W_PAIRS
+                    words.append(
+                        load_words(nc, weights, fc_w_words, next_pair, singly=next_pair == BANDS * GROUPS - 2)
+                    )
+            width = STORE_TILES[band] * N_TILE
+            for m in range(EMB // width):
+                result = io.tile([P, width], F32, tag="io", name="result%d_%d" % (band, m))
+                for h in range(STORE_TILES[band]):
+                    n = m * STORE_TILES[band] + h
                     bias_cols = slice(band * EMB + n * N_TILE, band * EMB + (n + 1) * N_TILE)
                     nc.vector.tensor_tensor(
                         out=result[:, h * N_TILE : (h + 1) * N_TILE], in0=acc[n][:], in1=bias[:, bias_cols], op=ALU.add
                     )
-                stored = slice(m * STORE_TILES * N_TILE, (m + 1) * STORE_TILES * N_TILE)
-                nc.sync.dma_start(out=out[0, band, :, stored], in_=result[:])
+                nc.sync.dma_start(out=out[0, band, :, m * width : (m + 1) * width], in_=result[:])

@@ -31,8 +31,10 @@ N_TILE = 512
 N_TILES = EMB // N_TILE
 PLANES = 4
 QUADRANTS = 4
-W_PAIRS = 5
-STORE_TILES = (3, 2)
+W_BUFS = 10
+FIRST_LOADS = ((0, 4), (4, 4), (8, 2))
+NEXT_LOADS = {1: (10, 2), 3: (12, 2), 4: (14, 1)}
+STORE_TILES = (6, 2)
 
 GAIN_ROW = 0
 SHIFT_ROW = BANDS * GROUPS
@@ -41,14 +43,12 @@ FC_B_ROW = 2 * BANDS * GROUPS
 FLOPS = 2 * BANDS * FRAMES * FEAT * EMB
 
 
-def load_words(nc, pool, fc_w_words, k, singly=False):
-    words = pool.tile([P, 2, EMB], U32, tag="words", name="words%d" % k, align_bytes=64)
-    for first, count in ((0, 1), (1, 1)) if singly else ((0, 2),):
-        nc.sync.dma_start(
-            out=words[:, first : first + count, :].bitcast(I32),
-            in_=fc_w_words[k + first : k + first + count].rearrange("g p n t -> p g (n t)").bitcast(I32),
-        )
-    return words
+def load_words(nc, words, fc_w_words, first, count, cols=slice(0, EMB)):
+    place = first % W_BUFS
+    nc.sync.dma_start(
+        out=words[:, place : place + count, cols].bitcast(I32),
+        in_=fc_w_words[first : first + count, :, cols, :].rearrange("g p n t -> p g (n t)").bitcast(I32),
+    )
 
 
 def to_frames_first(nc, ln, acc_pool, x_rows, xt, sums, ident_bf):
@@ -58,7 +58,7 @@ def to_frames_first(nc, ln, acc_pool, x_rows, xt, sums, ident_bf):
             for u in range(2):
                 turned = acc_pool.tile([P, ROW_BINS // 2, P], BF16, tag="acc")
                 for b in range(ROW_BINS // 2):
-                    nc.tensor.transpose(out=turned[:, b, :], in_=x_rows[r][:, c, 2 * b + u, :], identity=ident_bf)
+                    nc.tensor.transpose(out=turned[:, b, :], in_=x_rows[:, r, c, 2 * b + u, :], identity=ident_bf)
                 nc.scalar.copy(
                     out=xt[:, :, c, u, r, :].rearrange("t n (i b) -> t n i b", b=ROW_BINS // 2),
                     in_=turned[:].rearrange("t b (n i) -> t n i b", n=RUNS),
@@ -131,21 +131,21 @@ def tile_bandsplitmodule_w_e_kernel(tc, x_real, x_imag, ln_w, ln_b, fc_w_words, 
     nc = tc.nc
     with ExitStack() as stack:
         const = stack.enter_context(tc.tile_pool(name="const", bufs=1))
-        weights = stack.enter_context(tc.tile_pool(name="weights", bufs=W_PAIRS))
-        io = stack.enter_context(tc.tile_pool(name="io", bufs=4))
+        io = stack.enter_context(tc.tile_pool(name="io", bufs=1))
         ln = stack.enter_context(tc.tile_pool(name="ln", bufs=2))
         acc_pool = stack.enter_context(tc.psum_pool(name="acc", bufs=N_TILES))
         stat_pool = stack.enter_context(tc.psum_pool(name="stat", bufs=2))
         stack.enter_context(tc.manual_schedule())
 
-        x_rows = []
+        x_rows = io.tile([P, PARTS, CHANNELS, ROW_BINS, FRAMES], BF16, tag="io", name="x_rows")
         for r, x_part in enumerate((x_real, x_imag)):
-            x_rows.append(io.tile([P, CHANNELS, ROW_BINS, FRAMES], BF16, tag="io", name="x_rows%d" % r))
             nc.sync.dma_start(
-                out=x_rows[r][:].rearrange("q c b t -> q c (b t)"),
+                out=x_rows[:, r, :, :, :].rearrange("q c b t -> q c (b t)"),
                 in_=x_part[0].rearrange("c (q b) t -> q c (b t)", b=ROW_BINS),
             )
-        words = [load_words(nc, weights, fc_w_words, 2 * i) for i in range(W_PAIRS)]
+        words = const.tile([P, W_BUFS, EMB], U32, align_bytes=64)
+        for first, count in FIRST_LOADS:
+            load_words(nc, words, fc_w_words, first, count)
 
         small = const.tile([P, K_PASS], BF16)
         nc.vector.memset(small[:], 0.0)
@@ -246,23 +246,22 @@ def tile_bandsplitmodule_w_e_kernel(tc, x_real, x_imag, ln_w, ln_b, fc_w_words, 
                         out=acc[n][:],
                         lhsT=codes[band][:, frames].bitcast(FP8X4),
                         lhsT_scale=code_scales[band][:, frames],
-                        rhs=words[k // 2][:, k % 2, cols].bitcast(FP8X4),
+                        rhs=words[:, k % W_BUFS, cols].bitcast(FP8X4),
                         rhs_scale=planes[4 * b : P, a, cols],
                         start=(g == 0),
                         stop=(g == GROUPS - 1),
                     )
-                if k % 2 == 1 and k + 2 * W_PAIRS < BANDS * GROUPS:
-                    next_pair = k - 1 + 2 * W_PAIRS
-                    words.append(
-                        load_words(nc, weights, fc_w_words, next_pair, singly=next_pair == BANDS * GROUPS - 2)
-                    )
-            width = STORE_TILES[band] * N_TILE
-            for m in range(EMB // width):
-                result = io.tile([P, width], F32, tag="io", name="result%d_%d" % (band, m))
-                for h in range(STORE_TILES[band]):
-                    n = m * STORE_TILES[band] + h
-                    bias_cols = slice(band * EMB + n * N_TILE, band * EMB + (n + 1) * N_TILE)
-                    nc.vector.tensor_tensor(
-                        out=result[:, h * N_TILE : (h + 1) * N_TILE], in0=acc[n][:], in1=bias[:, bias_cols], op=ALU.add
-                    )
-                nc.sync.dma_start(out=out[0, band, :, m * width : (m + 1) * width], in_=result[:])
+                if band == 0 and g in NEXT_LOADS:
+                    load_words(nc, words, fc_w_words, *NEXT_LOADS[g])
+                if band == 0 and g == 5:
+                    width = STORE_TILES[1] * N_TILE
+                    for first in range(0, EMB, width):
+                        load_words(nc, words, fc_w_words, BANDS * GROUPS - 1, 1, slice(first, first + width))
+            result = io.tile([P, EMB], F32, tag=("result", "io")[band], name="result%d" % band)
+            for n in range(N_TILES):
+                cols = slice(n * N_TILE, (n + 1) * N_TILE)
+                bias_cols = slice(band * EMB + n * N_TILE, band * EMB + (n + 1) * N_TILE)
+                nc.vector.tensor_tensor(out=result[:, cols], in0=acc[n][:], in1=bias[:, bias_cols], op=ALU.add)
+                if (n + 1) % STORE_TILES[band] == 0:
+                    stored = slice((n + 1 - STORE_TILES[band]) * N_TILE, (n + 1) * N_TILE)
+                    nc.sync.dma_start(out=out[0, band, :, stored], in_=result[:, stored])

@@ -51,6 +51,14 @@ def load_words(nc, words, fc_w_words, first, count, cols=slice(0, EMB)):
     )
 
 
+def load_scales(nc, planes, fc_w_scales, a):
+    for quadrant in range(QUADRANTS):
+        nc.sync.dma_start(
+            out=planes[32 * quadrant : 32 * quadrant + 4 * PLANES, a, :].bitcast(I32),
+            in_=fc_w_scales[PLANES * a : PLANES * (a + 1), 4 * quadrant : 4 * (quadrant + 1), :].bitcast(I32),
+        )
+
+
 def to_frames_first(nc, ln, acc_pool, x_rows, xt, sums, ident_bf):
     i = 0
     for r in range(PARTS):
@@ -137,27 +145,28 @@ def tile_bandsplitmodule_w_e_kernel(tc, x_real, x_imag, ln_w, ln_b, fc_w_words, 
         stat_pool = stack.enter_context(tc.psum_pool(name="stat", bufs=2))
         stack.enter_context(tc.manual_schedule())
 
+        small = const.tile([P, K_PASS], BF16)
+        nc.vector.memset(small[:], 0.0)
+        planes = const.tile([P, PLANES, EMB], U8, align_bytes=64)
+        nc.vector.memset(planes[:].rearrange("p a n -> p (a n)").bitcast(I32), 0)
+
         x_rows = io.tile([P, PARTS, CHANNELS, ROW_BINS, FRAMES], BF16, tag="io", name="x_rows")
         for r, x_part in enumerate((x_real, x_imag)):
             nc.sync.dma_start(
                 out=x_rows[:, r, :, :, :].rearrange("q c b t -> q c (b t)"),
                 in_=x_part[0].rearrange("c (q b) t -> q c (b t)", b=ROW_BINS),
             )
+        for first, rows, values in (
+            (GAIN_ROW, BANDS * GROUPS, ln_w.rearrange("n (g k) -> (n g) k", k=K_PASS)),
+            (SHIFT_ROW, BANDS * GROUPS, ln_b.rearrange("n (g k) -> (n g) k", k=K_PASS)),
+            (FC_B_ROW, BANDS * N_TILES, fc_b.rearrange("n (c e) -> (n c) e", e=N_TILE)),
+        ):
+            nc.sync.dma_start(out=small[first : first + rows, :], in_=values)
         words = const.tile([P, W_BUFS, EMB], U32, align_bytes=64)
+        for a in range(PLANES):
+            load_scales(nc, planes, fc_w_scales, a)
         for first, count in FIRST_LOADS:
             load_words(nc, words, fc_w_words, first, count)
-
-        small = const.tile([P, K_PASS], BF16)
-        nc.vector.memset(small[:], 0.0)
-        nc.scalar.dma_start(
-            out=small[GAIN_ROW : GAIN_ROW + BANDS * GROUPS, :], in_=ln_w.rearrange("n (g k) -> (n g) k", k=K_PASS)
-        )
-        nc.scalar.dma_start(
-            out=small[SHIFT_ROW : SHIFT_ROW + BANDS * GROUPS, :], in_=ln_b.rearrange("n (g k) -> (n g) k", k=K_PASS)
-        )
-        nc.scalar.dma_start(
-            out=small[FC_B_ROW : FC_B_ROW + BANDS * N_TILES, :], in_=fc_b.rearrange("n (c e) -> (n c) e", e=N_TILE)
-        )
 
         ident_bf = const.tile([P, P], BF16)
         make_identity(nc, ident_bf[:])
@@ -168,15 +177,6 @@ def tile_bandsplitmodule_w_e_kernel(tc, x_real, x_imag, ln_w, ln_b, fc_w_words, 
 
         first_table = const.tile([P, 1], F32)
         nc.scalar.sqrt(out=first_table[:], in_=ones_f32[:])
-
-        planes = const.tile([P, PLANES, EMB], U8, align_bytes=64)
-        nc.vector.memset(planes[:].rearrange("p a n -> p (a n)").bitcast(I32), 0)
-        for a in range(BANDS * GROUPS // PLANES):
-            for quadrant in range(QUADRANTS):
-                nc.gpsimd.dma_start(
-                    out=planes[32 * quadrant : 32 * quadrant + 4 * PLANES, a, :].bitcast(F32),
-                    in_=fc_w_scales[PLANES * a : PLANES * (a + 1), 4 * quadrant : 4 * (quadrant + 1), :].bitcast(F32),
-                )
 
         xt = const.tile([P, RUNS, CHANNELS, 2, PARTS, P], BF16)
         sums = const.tile([P, BANDS, CHANNELS * PARTS * 2, 6], F32)

@@ -53,9 +53,10 @@ def load_words(nc, words, fc_w_words, first, count, cols=slice(0, EMB)):
 
 def load_scales(nc, planes, fc_w_scales, a):
     for quadrant in range(QUADRANTS):
-        nc.sync.dma_start(
-            out=planes[32 * quadrant : 32 * quadrant + 4 * PLANES, a, :].bitcast(I32),
-            in_=fc_w_scales[PLANES * a : PLANES * (a + 1), 4 * quadrant : 4 * (quadrant + 1), :].bitcast(I32),
+        queue, dtype = ((nc.sync, I32), (nc.gpsimd, F32))[quadrant // 2]
+        queue.dma_start(
+            out=planes[32 * quadrant : 32 * quadrant + 4 * PLANES, a, :].bitcast(dtype),
+            in_=fc_w_scales[PLANES * a : PLANES * (a + 1), 4 * quadrant : 4 * (quadrant + 1), :].bitcast(dtype),
         )
 
 
@@ -150,6 +151,10 @@ def tile_bandsplitmodule_w_e_kernel(tc, x_real, x_imag, ln_w, ln_b, fc_w_words, 
         planes = const.tile([P, PLANES, EMB], U8, align_bytes=64)
         nc.vector.memset(planes[:].rearrange("p a n -> p (a n)").bitcast(I32), 0)
 
+        ident_bf = const.tile([P, P], BF16)
+        make_identity(nc, ident_bf[:])
+        ident_f32 = const.tile([P, P], F32)
+        make_identity(nc, ident_f32[:])
         x_rows = io.tile([P, PARTS, CHANNELS, ROW_BINS, FRAMES], BF16, tag="io", name="x_rows")
         for r, x_part in enumerate((x_real, x_imag)):
             nc.sync.dma_start(
@@ -168,10 +173,6 @@ def tile_bandsplitmodule_w_e_kernel(tc, x_real, x_imag, ln_w, ln_b, fc_w_words, 
         for first, count in FIRST_LOADS:
             load_words(nc, words, fc_w_words, first, count)
 
-        ident_bf = const.tile([P, P], BF16)
-        make_identity(nc, ident_bf[:])
-        ident_f32 = const.tile([P, P], F32)
-        make_identity(nc, ident_f32[:])
         ones_f32 = const.tile([P, 1], F32)
         nc.vector.memset(ones_f32[:], 1.0)
 

@@ -146,15 +146,15 @@ def tile_bandsplitmodule_w_e_kernel(tc, x_real, x_imag, ln_w, ln_b, fc_w_words, 
         stat_pool = stack.enter_context(tc.psum_pool(name="stat", bufs=2))
         stack.enter_context(tc.manual_schedule())
 
-        small = const.tile([P, K_PASS], BF16)
-        nc.vector.memset(small[:], 0.0)
         planes = const.tile([P, PLANES, EMB], U8, align_bytes=64)
-        nc.vector.memset(planes[:].rearrange("p a n -> p (a n)").bitcast(I32), 0)
+        small = const.tile([P, K_PASS], BF16)
+        for a in range(PLANES):
+            nc.vector.memset(planes[:, a, :].bitcast(I32), 0)
+            if a == 0:
+                nc.vector.memset(small[:], 0.0)
 
         ident_bf = const.tile([P, P], BF16)
         make_identity(nc, ident_bf[:])
-        ident_f32 = const.tile([P, P], F32)
-        make_identity(nc, ident_f32[:])
         x_rows = io.tile([P, PARTS, CHANNELS, ROW_BINS, FRAMES], BF16, tag="io", name="x_rows")
         for r, x_part in enumerate((x_real, x_imag)):
             nc.sync.dma_start(
@@ -173,6 +173,8 @@ def tile_bandsplitmodule_w_e_kernel(tc, x_real, x_imag, ln_w, ln_b, fc_w_words, 
         for first, count in FIRST_LOADS:
             load_words(nc, words, fc_w_words, first, count)
 
+        ident_f32 = const.tile([P, P], F32)
+        make_identity(nc, ident_f32[:])
         ones_f32 = const.tile([P, 1], F32)
         nc.vector.memset(ones_f32[:], 1.0)
 

from contextlib import ExitStack

import concourse.mybir as mybir
from concourse.masks import make_identity

F32 = mybir.dt.float32
BF16 = mybir.dt.bfloat16
I32 = mybir.dt.int32
U32 = mybir.dt.uint32
U8 = mybir.dt.uint8
FP8X4 = mybir.dt.float8_e4m3fn_x4
ALU = mybir.AluOpType
ACT = mybir.ActivationFunctionType

P = 128
PACK = 4
K_PASS = P * PACK
BANDS = 2
CHANNELS = 2
PARTS = 2
BINS = 1024
FRAMES = 128
FEAT = CHANNELS * BINS * PARTS
EMB = 3072
EPS = 1e-5
GROUPS = FEAT // K_PASS
GROUPS_C = GROUPS // CHANNELS
RUNS = BANDS * GROUPS_C
ROW_BINS = BANDS * BINS // P
N_TILE = 512
N_TILES = EMB // N_TILE
PLANES = 4
QUADRANTS = 4
W_BUFS = 10
FIRST_LOADS = ((0, 4), (4, 4), (8, 2))
NEXT_LOADS = {1: (10, 2), 3: (12, 2), 4: (14, 1)}
STORE_TILES = (6, 2)

GAIN_ROW = 0
SHIFT_ROW = BANDS * GROUPS
FC_B_ROW = 2 * BANDS * GROUPS

FLOPS = 2 * BANDS * FRAMES * FEAT * EMB


def load_words(nc, words, fc_w_words, first, count, cols=slice(0, EMB)):
    place = first % W_BUFS
    nc.sync.dma_start(
        out=words[:, place : place + count, cols].bitcast(I32),
        in_=fc_w_words[first : first + count, :, cols, :].rearrange("g p n t -> p g (n t)").bitcast(I32),
    )


def load_scales(nc, planes, fc_w_scales, a):
    for quadrant in range(QUADRANTS):
        queue, dtype = ((nc.sync, I32), (nc.gpsimd, F32))[quadrant // 2]
        queue.dma_start(
            out=planes[32 * quadrant : 32 * quadrant + 4 * PLANES, a, :].bitcast(dtype),
            in_=fc_w_scales[PLANES * a : PLANES * (a + 1), 4 * quadrant : 4 * (quadrant + 1), :].bitcast(dtype),
        )


def to_frames_first(nc, ln, acc_pool, x_rows, xt, sums, ident_bf):
    i = 0
    for r in range(PARTS):
        for c in range(CHANNELS):
            for u in range(2):
                turned = acc_pool.tile([P, ROW_BINS // 2, P], BF16, tag="acc")
                for b in range(ROW_BINS // 2):
                    nc.tensor.transpose(out=turned[:, b, :], in_=x_rows[:, r, c, 2 * b + u, :], identity=ident_bf)
                nc.scalar.copy(
                    out=xt[:, :, c, u, r, :].rearrange("t n (i b) -> t n i b", b=ROW_BINS // 2),
                    in_=turned[:].rearrange("t b (n i) -> t n i b", n=RUNS),
                )
                for band in range(BANDS):
                    half = slice(band * P // BANDS, (band + 1) * P // BANDS)
                    nc.vector.bn_stats(out=sums[:, band, i, :], in_=turned[:, :, half])
                i += 1


def normalise(nc, ln, band, c, xt, stats, rstd):
    y = ln.tile([P, GROUPS_C, PACK, P], F32, tag="y")
    nc.vector.tensor_scalar(
        out=y[:].rearrange("t g j p -> t g (j p)"),
        in0=xt[:, band * GROUPS_C : (band + 1) * GROUPS_C, c, :, :, :].rearrange("t g u r p -> t g (u r p)"),
        scalar1=stats[:, band, 0:1],
        scalar2=rstd[:, band : band + 1],
        op0=ALU.subtract,
        op1=ALU.mult,
    )
    return y


def back_to_features_first(nc, pool, tag, band, c, g, y, xn, params, ident_f32):
    back = pool.tile([P, PACK, FRAMES], F32, tag=tag)
    for j in range(PACK):
        nc.tensor.transpose(out=back[:, j, :], in_=y[:, g, j, :], identity=ident_f32)
    row = band * GROUPS + c * GROUPS_C + g
    for j in range(PACK):
        gain = params[:, j, GAIN_ROW + row : GAIN_ROW + row + 1]
        shift = params[:, j, SHIFT_ROW + row : SHIFT_ROW + row + 1]
        if g % 2 == 0:
            nc.scalar.activation(out=xn[:, g, j, :], in_=back[:, j, :], func=ACT.Identity, scale=gain, bias=shift)
        else:
            nc.vector.tensor_scalar(
                out=xn[:, g, j, :], in0=back[:, j, :], scalar1=gain, scalar2=shift, op0=ALU.mult, op1=ALU.add
            )


def interleave(nc, ln, xn):
    grouped = ln.tile([P, GROUPS_C, FRAMES, PACK], BF16, tag="grouped", align_bytes=64)
    nc.vector.tensor_copy(out=grouped[:], in_=xn[:].rearrange("p g j t -> p g t j"))
    return grouped


def quantise(nc, c, grouped, codes, code_scales):
    columns = slice(c * GROUPS_C * FRAMES, (c + 1) * GROUPS_C * FRAMES)
    nc.vector.quantize_mx(
        out=codes[:, columns].bitcast(FP8X4),
        scales=code_scales[:, columns],
        in_=grouped[:].rearrange("p g t j -> p (g t j)"),
    )


def spread_bias(nc, stat_pool, small, ident_bf, bias, i):
    bias_ps = stat_pool.tile([P, 2, N_TILE], BF16, tag="stat")
    for h in range(2):
        row = FC_B_ROW + 2 * i + h
        nc.tensor.matmul(
            out=bias_ps[:, h, :],
            lhsT=ident_bf[:, row : row + 1].to_broadcast([P, P]),
            rhs=small[:],
            start=True,
            stop=True,
        )
    nc.scalar.copy(out=bias[:, 2 * i * N_TILE : 2 * (i + 1) * N_TILE], in_=bias_ps[:].rearrange("p h n -> p (h n)"))


def tile_bandsplitmodule_w_e_kernel(tc, x_real, x_imag, ln_w, ln_b, fc_w_words, fc_w_scales, fc_b, out):
    nc = tc.nc
    with ExitStack() as stack:
        const = stack.enter_context(tc.tile_pool(name="const", bufs=1))
        io = stack.enter_context(tc.tile_pool(name="io", bufs=1))
        ln = stack.enter_context(tc.tile_pool(name="ln", bufs=2))
        acc_pool = stack.enter_context(tc.psum_pool(name="acc", bufs=N_TILES))
        stat_pool = stack.enter_context(tc.psum_pool(name="stat", bufs=2))
        stack.enter_context(tc.manual_schedule())

        planes = const.tile([P, PLANES, EMB], U8, align_bytes=64)
        small = const.tile([P, K_PASS], BF16)
        for a in range(PLANES):
            nc.vector.memset(planes[:, a, :].bitcast(I32), 0)
            if a == 0:
                nc.vector.memset(small[:], 0.0)

        ident_bf = const.tile([P, P], BF16)
        make_identity(nc, ident_bf[:])
        x_rows = io.tile([P, PARTS, CHANNELS, ROW_BINS, FRAMES], BF16, tag="io", name="x_rows")
        for r, x_part in enumerate((x_real, x_imag)):
            nc.sync.dma_start(
                out=x_rows[:, r, :, :, :].rearrange("q c b t -> q c (b t)"),
                in_=x_part[0].rearrange("c (q b) t -> q c (b t)", b=ROW_BINS),
            )
        for first, rows, values in (
            (GAIN_ROW, BANDS * GROUPS, ln_w.rearrange("n (g k) -> (n g) k", k=K_PASS)),
            (SHIFT_ROW, BANDS * GROUPS, ln_b.rearrange("n (g k) -> (n g) k", k=K_PASS)),
            (FC_B_ROW, BANDS * N_TILES, fc_b.rearrange("n (c e) -> (n c) e", e=N_TILE)),
        ):
            nc.sync.dma_start(out=small[first : first + rows, :], in_=values)
        words = const.tile([P, W_BUFS, EMB], U32, align_bytes=64)
        for a in range(PLANES):
            load_scales(nc, planes, fc_w_scales, a)
        for first, count in FIRST_LOADS:
            load_words(nc, words, fc_w_words, first, count)

        ident_f32 = const.tile([P, P], F32)
        make_identity(nc, ident_f32[:])
        ones_f32 = const.tile([P, 1], F32)
        nc.vector.memset(ones_f32[:], 1.0)

        first_table = const.tile([P, 1], F32)
        nc.scalar.sqrt(out=first_table[:], in_=ones_f32[:])

        xt = const.tile([P, RUNS, CHANNELS, 2, PARTS, P], BF16)
        sums = const.tile([P, BANDS, CHANNELS * PARTS * 2, 6], F32)
        to_frames_first(nc, ln, acc_pool, x_rows, xt, sums, ident_bf[:])

        params_ps = stat_pool.tile([P, PACK, P], BF16, tag="stat")
        for j in range(PACK):
            nc.tensor.transpose(out=params_ps[:, j, :], in_=small[:, j:K_PASS:PACK], identity=ident_bf[:])
        params = const.tile([P, PACK, FC_B_ROW], F32)
        nc.scalar.copy(out=params[:], in_=params_ps[:, :, 0:FC_B_ROW])

        stats = const.tile([P, BANDS, 2], F32)
        for band in range(BANDS):
            nc.vector.bn_aggr(out=stats[:, band, :], in_=sums[:, band, :, :].rearrange("t i s -> t (i s)"))
        var_eps = const.tile([P, BANDS], F32)
        nc.vector.tensor_scalar_add(out=var_eps[:], in0=stats[:, :, 1], scalar1=EPS)
        inverse = const.tile([P, BANDS], F32)
        nc.vector.reciprocal(out=inverse[:], in_=var_eps[:])
        rstd = const.tile([P, BANDS], F32)
        nc.scalar.sqrt(out=rstd[:], in_=inverse[:])

        bias = const.tile([P, BANDS * EMB], BF16)

        codes = [const.tile([P, GROUPS * FRAMES], U32, name="codes%d" % band, align_bytes=64) for band in range(BANDS)]
        code_scales = [
            const.tile([P, GROUPS * FRAMES], U8, name="code_scales%d" % band, align_bytes=64) for band in range(BANDS)
        ]

        steps = [(band, c) for band in range(BANDS) for c in range(CHANNELS)]
        ys = {}
        xns = {}

        def turn_back(i):
            band, c = steps[i]
            xns[i] = ln.tile([P, GROUPS_C, PACK, FRAMES], BF16, tag="xn", name="xn%d" % i)
            pool, tag = (acc_pool, "acc") if band == 0 else (stat_pool, "stat")
            for g in range(GROUPS_C):
                back_to_features_first(nc, pool, tag, band, c, g, ys[i], xns[i], params, ident_f32[:])

        def finish(i):
            band, c = steps[i]
            grouped = interleave(nc, ln, xns[i])
            if i + 2 < len(steps):
                ys[i + 2] = normalise(nc, ln, *steps[i + 2], xt, stats, rstd)
            quantise(nc, c, grouped, codes[band], code_scales[band])

        for i in range(2):
            ys[i] = normalise(nc, ln, *steps[i], xt, stats, rstd)
        for i in range(3):
            turn_back(i)
            finish(i)

        for band in range(BANDS):
            acc = [acc_pool.tile([P, N_TILE], F32, tag="acc", name="acc%d_%d" % (band, n)) for n in range(N_TILES)]
            for g in range(GROUPS):
                if band == 0 and g == 2:
                    turn_back(3)
                    finish(3)
                if band == 0 and g >= 2:
                    spread_bias(nc, stat_pool, small, ident_bf, bias, g - 2)
                k = band * GROUPS + g
                a, b = divmod(k, PLANES)
                frames = slice(g * FRAMES, (g + 1) * FRAMES)
                for n in range(N_TILES):
                    cols = slice(n * N_TILE, (n + 1) * N_TILE)
                    nc.tensor.matmul_mx(
                        out=acc[n][:],
                        lhsT=codes[band][:, frames].bitcast(FP8X4),
                        lhsT_scale=code_scales[band][:, frames],
                        rhs=words[:, k % W_BUFS, cols].bitcast(FP8X4),
                        rhs_scale=planes[4 * b : P, a, cols],
                        start=(g == 0),
                        stop=(g == GROUPS - 1),
                    )
                if band == 0 and g in NEXT_LOADS:
                    load_words(nc, words, fc_w_words, *NEXT_LOADS[g])
                if band == 0 and g == 5:
                    width = STORE_TILES[1] * N_TILE
                    for first in range(0, EMB, width):
                        load_words(nc, words, fc_w_words, BANDS * GROUPS - 1, 1, slice(first, first + width))
            result = io.tile([P, EMB], F32, tag=("result", "io")[band], name="result%d" % band)
            for n in range(N_TILES):
                cols = slice(n * N_TILE, (n + 1) * N_TILE)
                bias_cols = slice(band * EMB + n * N_TILE, band * EMB + (n + 1) * N_TILE)
                nc.vector.tensor_tensor(out=result[:, cols], in0=acc[n][:], in1=bias[:, bias_cols], op=ALU.add)
                if (n + 1) % STORE_TILES[band] == 0:
                    stored = slice((n + 1 - STORE_TILES[band]) * N_TILE, (n + 1) * N_TILE)
                    nc.sync.dma_start(out=out[0, band, :, stored], in_=result[:, stored])
